import numpy as np
import ml_dtypes

BF16 = ml_dtypes.bfloat16


def bf(x):
    return np.asarray(x, np.float32).astype(BF16)


def f32(x):
    return np.asarray(x, np.float32)


def f64(x):
    return np.asarray(x).astype(np.float64)


def striped(idx):
    return np.tile(idx.reshape(-1, 16).T, (8, 1))


C, CH, M, S, HH, WW, N = 512, 256, 1536, 2048, 32, 32, 1024


def setup_inputs():
    return {"table": f32(np.random.standard_normal((C, S))), "row_embed": f32(0.5 * np.random.standard_normal((CH, HH))), "col_embed": f32(0.5 * np.random.standard_normal((CH, WW))), "wqkv": bf(np.random.standard_normal((C, M)) / np.sqrt(C)), "bqkv": f32(0.1 * np.random.standard_normal((M, 1))), "offs": striped(np.random.permutation(np.tile(np.arange(S), 2))[:N])}


def reference(table, row_embed, col_embed, wqkv, bqkv, offs):
    idx = offs[:16].T.reshape(-1)
    pos = np.concatenate([np.repeat(f64(row_embed), WW, axis=1), np.tile(f64(col_embed), (1, HH))], axis=0)
    h = f64(table)[:, idx] + pos
    qkv = f64(wqkv).T @ h + f64(bqkv)
    return np.concatenate([h, qkv], axis=0)

@@ -1,0 +1,101 @@
+import concourse.mybir as mybir
+from concourse.masks import make_identity
+
+F32, BF16, U16 = mybir.dt.float32, mybir.dt.bfloat16, mybir.dt.uint16
+ADD = mybir.AluOpType.add
+COPY = mybir.ActivationFunctionType.Copy
+IDENTITY = mybir.ActivationFunctionType.Identity
+
+P = 128
+C = 512
+M = 1536
+S = 2048
+GRID = 32
+N = GRID * GRID
+BANK = 512
+KB = C // P
+MB = M // P
+JB = N // BANK
+
+FLOPS = 2 * C * M * N
+
+
+def tile_autoregressivemodel_kernel(tc, table, row_embed, col_embed, wqkv, bqkv, offs, out):
+    nc = tc.nc
+    with (
+        tc.tile_pool(name="held", bufs=1) as held,
+        tc.tile_pool(name="staging", bufs=6) as staging,
+    ):
+        offsets = held.tile([P, N // 16], U16, name="offsets")
+        nc.sync.dma_start(offsets[:], offs)
+
+        positions = []
+        for k in range(KB):
+            code = held.tile([P, GRID], F32, name=f"code{k}")
+            pos = held.tile([P, N], F32, name=f"pos{k}")
+            if k < KB // 2:
+                nc.scalar.dma_start(code[:], row_embed[k * P : (k + 1) * P, :])
+                spread = code[:].unsqueeze(2)
+            else:
+                nc.scalar.dma_start(code[:], col_embed[(k - KB // 2) * P : (k - KB // 2 + 1) * P, :])
+                spread = code[:].unsqueeze(1)
+            nc.gpsimd.tensor_copy(
+                pos[:].rearrange("p (r c) -> p r c", c=GRID), spread.to_broadcast([P, GRID, GRID])
+            )
+            positions.append(pos)
+
+        tables, weights = [], []
+        for k in range(KB):
+            window = held.tile([P, S], F32, name=f"table{k}")
+            nc.sync.dma_start(window[:], table[k * P : (k + 1) * P, :])
+            tables.append(window)
+            weight = held.tile([P, M], BF16, name=f"weight{k}")
+            nc.sync.dma_start(weight[:], wqkv[k * P : (k + 1) * P, :])
+            weights.append(weight)
+
+        identity = held.tile([P, P], F32, name="identity")
+        make_identity(nc, identity[:])
+        bias_rows = held.tile([P, P], F32, name="bias_rows")
+        nc.gpsimd.memset(bias_rows[:], 0.0)
+        nc.scalar.dma_start(bias_rows[0:MB, :], bqkv.rearrange("(b p) o -> b (p o)", p=P))
+        bias = held.tile([P, MB], F32, name="bias")
+        with tc.psum_pool(name="setup", bufs=1) as setup:
+            flipped = setup.tile([P, P], F32, name="flipped")
+            nc.tensor.transpose(flipped[:], bias_rows[:], identity[:])
+            nc.vector.tensor_copy(bias[:], flipped[:, 0:MB])
+
+        h_bf16 = []
+        for k in range(KB):
+            h = held.tile([P, N], F32, name=f"h{k}")
+            rounded = held.tile([P, N], BF16, name=f"h_bf16_{k}")
+            for j in range(JB):
+                piece = slice(j * BANK, (j + 1) * BANK)
+                nc.vector.tensor_tensor(
+                    h[:, piece],
+                    tables[k][:].indirect(offsets[:, j * (BANK // 16) : (j + 1) * (BANK // 16)]),
+                    positions[k][:, piece],
+                    ADD,
+                )
+                nc.scalar.activation(rounded[:, piece], h[:, piece], COPY)
+            nc.sync.dma_start(out[k * P : (k + 1) * P, :], h[:])
+            h_bf16.append(rounded)
+
+        with tc.psum_pool(name="psum", bufs=8) as psum:
+            for m in range(MB):
+                for j in range(JB):
+                    piece = slice(j * BANK, (j + 1) * BANK)
+                    acc = psum.tile([P, BANK], F32, name="acc")
+                    for k in range(KB):
+                        nc.tensor.matmul(
+                            acc[:],
+                            weights[k][:, m * P : (m + 1) * P],
+                            h_bf16[k][:, piece],
+                            start=(k == 0),
+                            stop=(k == KB - 1),
+                        )
+                    qkv = staging.tile([P, BANK], F32, name="qkv")
+                    if j % 2 == 0:
+                        nc.scalar.activation(qkv[:], acc[:], IDENTITY, bias=bias[:, m : m + 1])
+                    else:
+                        nc.vector.tensor_scalar_add(qkv[:], acc[:], bias[:, m : m + 1])
+                    nc.sync.dma_start(out[C + m * P : C + (m + 1) * P, piece], qkv[:])

@@ -1,5 +1,4 @@
 import concourse.mybir as mybir
-from concourse.masks import make_identity
 
 F32, BF16, U16 = mybir.dt.float32, mybir.dt.bfloat16, mybir.dt.uint16
 ADD = mybir.AluOpType.add
@@ -13,9 +12,12 @@ S = 2048
 GRID = 32
 N = GRID * GRID
 BANK = 512
+BANKS = 8
 KB = C // P
-MB = M // P
 JB = N // BANK
+GROUPS = 3
+BLOCKS = C // P
+assert BLOCKS * JB == BANKS
 
 FLOPS = 2 * C * M * N
 
@@ -24,78 +26,87 @@ def tile_autoregressivemodel_kernel(tc, table, row_embed, col_embed, wqkv, bqkv,
     nc = tc.nc
     with (
         tc.tile_pool(name="held", bufs=1) as held,
-        tc.tile_pool(name="staging", bufs=6) as staging,
+        tc.tile_pool(name="staging", bufs=GROUPS * BLOCKS * JB) as staging,
+        tc.psum_pool(name="psum", bufs=BANKS) as psum,
     ):
+        codes = held.tile([P, KB, GRID], F32, name="codes")
+        nc.scalar.dma_start(codes[:, 0 : KB // 2, :], row_embed.rearrange("(k p) g -> p k g", p=P))
+        nc.scalar.dma_start(codes[:, KB // 2 : KB, :], col_embed.rearrange("(k p) g -> p k g", p=P))
+        bias = held.tile([P, GROUPS, BLOCKS], F32, name="bias")
+        nc.scalar.dma_start(bias[:], bqkv.rearrange("(g p b) o -> p g (b o)", g=GROUPS, b=BLOCKS))
+
         offsets = held.tile([P, N // 16], U16, name="offsets")
         nc.sync.dma_start(offsets[:], offs)
+        tables = [held.tile([P, S], F32, name=f"table{k}") for k in range(KB)]
+        weights = [held.tile([P, KB, C], BF16, name=f"weights{g}") for g in range(GROUPS)]
+        wqkv_of = wqkv.rearrange("(k c) (g m) -> g c k m", c=P, g=GROUPS)
+        nc.sync.dma_start(tables[0][:], table[0:P, :])
+        nc.sync.dma_start(weights[0][:], wqkv_of[0])
+        for k in range(1, KB):
+            nc.sync.dma_start(tables[k][:], table[k * P : (k + 1) * P, :])
+        for g in range(1, GROUPS):
+            nc.sync.dma_start(weights[g][:], wqkv_of[g])
+
+        weights_of = [weights[g][:].rearrange("c k (p b) -> c k b p", b=BLOCKS) for g in range(GROUPS)]
+        out_of = out[C : C + M, :].rearrange("(g p b) n -> g b p n", g=GROUPS, b=BLOCKS)
 
         positions = []
         for k in range(KB):
-            code = held.tile([P, GRID], F32, name=f"code{k}")
             pos = held.tile([P, N], F32, name=f"pos{k}")
+            pos_grid = pos[:].rearrange("p (r c) -> p r c", c=GRID)
             if k < KB // 2:
-                nc.scalar.dma_start(code[:], row_embed[k * P : (k + 1) * P, :])
-                spread = code[:].unsqueeze(2)
+                nc.scalar.activation(pos_grid, codes[:, k, :].unsqueeze(2).to_broadcast([P, GRID, GRID]), COPY)
             else:
-                nc.scalar.dma_start(code[:], col_embed[(k - KB // 2) * P : (k - KB // 2 + 1) * P, :])
-                spread = code[:].unsqueeze(1)
-            nc.gpsimd.tensor_copy(
-                pos[:].rearrange("p (r c) -> p r c", c=GRID), spread.to_broadcast([P, GRID, GRID])
-            )
+                nc.gpsimd.tensor_copy(pos_grid, codes[:, k, :].unsqueeze(1).to_broadcast([P, GRID, GRID]))
             positions.append(pos)
 
-        tables, weights = [], []
-        for k in range(KB):
-            window = held.tile([P, S], F32, name=f"table{k}")
-            nc.sync.dma_start(window[:], table[k * P : (k + 1) * P, :])
-            tables.append(window)
-            weight = held.tile([P, M], BF16, name=f"weight{k}")
-            nc.sync.dma_start(weight[:], wqkv[k * P : (k + 1) * P, :])
-            weights.append(weight)
+        h = [held.tile([P, N], F32, name=f"h{k}") for k in range(KB)]
+        h_bf16 = [held.tile([P, N], BF16, name=f"h_bf16_{k}") for k in range(KB)]
 
-        identity = held.tile([P, P], F32, name="identity")
-        make_identity(nc, identity[:])
-        bias_rows = held.tile([P, P], F32, name="bias_rows")
-        nc.gpsimd.memset(bias_rows[:], 0.0)
-        nc.scalar.dma_start(bias_rows[0:MB, :], bqkv.rearrange("(b p) o -> b (p o)", p=P))
-        bias = held.tile([P, MB], F32, name="bias")
-        with tc.psum_pool(name="setup", bufs=1) as setup:
-            flipped = setup.tile([P, P], F32, name="flipped")
-            nc.tensor.transpose(flipped[:], bias_rows[:], identity[:])
-            nc.vector.tensor_copy(bias[:], flipped[:, 0:MB])
+        def embed(k, j):
+            piece = slice(j * BANK, (j + 1) * BANK)
+            nc.vector.tensor_tensor(
+                h[k][:, piece],
+                tables[k][:].indirect(offsets[:, j * (BANK // 16) : (j + 1) * (BANK // 16)]),
+                positions[k][:, piece],
+                ADD,
+            )
+            nc.scalar.activation(h_bf16[k][:, piece], h[k][:, piece], COPY)
 
-        h_bf16 = []
+        def project(acc, g, b, j, k):
+            nc.tensor.matmul(
+                acc[:],
+                weights_of[g][:, k, b, :],
+                h_bf16[k][:, j * BANK : (j + 1) * BANK],
+                start=(k == 0),
+                stop=(k == KB - 1),
+            )
+
+        def finish(acc, g, b, j):
+            qkv = staging.tile([P, BANK], F32, name="qkv")
+            if j == 0:
+                nc.scalar.activation(qkv[:], acc[:], IDENTITY, bias=bias[:, g, b : b + 1])
+            else:
+                nc.vector.tensor_scalar_add(qkv[:], acc[:], bias[:, g, b : b + 1])
+            nc.sync.dma_start(out_of[g, b, :, j * BANK : (j + 1) * BANK], qkv[:])
+
+        queries = {}
         for k in range(KB):
-            h = held.tile([P, N], F32, name=f"h{k}")
-            rounded = held.tile([P, N], BF16, name=f"h_bf16_{k}")
             for j in range(JB):
-                piece = slice(j * BANK, (j + 1) * BANK)
-                nc.vector.tensor_tensor(
-                    h[:, piece],
-                    tables[k][:].indirect(offsets[:, j * (BANK // 16) : (j + 1) * (BANK // 16)]),
-                    positions[k][:, piece],
-                    ADD,
-                )
-                nc.scalar.activation(rounded[:, piece], h[:, piece], COPY)
-            nc.sync.dma_start(out[k * P : (k + 1) * P, :], h[:])
-            h_bf16.append(rounded)
+                embed(k, j)
+                for b in range(BLOCKS):
+                    if k == 0:
+                        queries[b, j] = psum.tile([P, BANK], F32, name="acc")
+                    project(queries[b, j], 0, b, j, k)
+            nc.sync.dma_start(out[k * P : (k + 1) * P, :], h[k][:])
+        for j in range(JB):
+            for b in range(BLOCKS):
+                finish(queries[b, j], 0, b, j)
 
-        with tc.psum_pool(name="psum", bufs=8) as psum:
-            for m in range(MB):
+        for g in range(1, GROUPS):
+            for b in range(BLOCKS):
                 for j in range(JB):
-                    piece = slice(j * BANK, (j + 1) * BANK)
                     acc = psum.tile([P, BANK], F32, name="acc")
                     for k in range(KB):
-                        nc.tensor.matmul(
-                            acc[:],
-                            weights[k][:, m * P : (m + 1) * P],
-                            h_bf16[k][:, piece],
-                            start=(k == 0),
-                            stop=(k == KB - 1),
-                        )
-                    qkv = staging.tile([P, BANK], F32, name="qkv")
-                    if j % 2 == 0:
-                        nc.scalar.activation(qkv[:], acc[:], IDENTITY, bias=bias[:, m : m + 1])
-                    else:
-                        nc.vector.tensor_scalar_add(qkv[:], acc[:], bias[:, m : m + 1])
-                    nc.sync.dma_start(out[C + m * P : C + (m + 1) * P, piece], qkv[:])
+                        project(acc, g, b, j, k)
+                    finish(acc, g, b, j)

@@ -18,6 +18,7 @@ JB = N // BANK
 GROUPS = 3
 BLOCKS = C // P
 assert BLOCKS * JB == BANKS
+WARMING = 16
 
 FLOPS = 2 * C * M * N
 
@@ -38,16 +39,18 @@ def tile_autoregressivemodel_kernel(tc, table, row_embed, col_embed, wqkv, bqkv,
         offsets = held.tile([P, N // 16], U16, name="offsets")
         nc.sync.dma_start(offsets[:], offs)
         tables = [held.tile([P, S], F32, name=f"table{k}") for k in range(KB)]
-        weights = [held.tile([P, KB, C], BF16, name=f"weights{g}") for g in range(GROUPS)]
-        wqkv_of = wqkv.rearrange("(k c) (g m) -> g c k m", c=P, g=GROUPS)
-        nc.sync.dma_start(tables[0][:], table[0:P, :])
-        nc.sync.dma_start(weights[0][:], wqkv_of[0])
-        for k in range(1, KB):
-            nc.sync.dma_start(tables[k][:], table[k * P : (k + 1) * P, :])
-        for g in range(1, GROUPS):
-            nc.sync.dma_start(weights[g][:], wqkv_of[g])
+        weights = [[held.tile([P, C], BF16, name=f"weights{g}_{k}") for k in range(KB)] for g in range(GROUPS)]
 
-        weights_of = [weights[g][:].rearrange("c k (p b) -> c k b p", b=BLOCKS) for g in range(GROUPS)]
+        def load_weights(g, k):
+            nc.sync.dma_start(weights[g][k][:], wqkv[k * P : (k + 1) * P, g * C : (g + 1) * C])
+
+        for k in range(KB):
+            nc.sync.dma_start(tables[k][:], table[k * P : (k + 1) * P, :])
+            load_weights(0, k)
+        for g in range(1, GROUPS):
+            for k in range(KB):
+                load_weights(g, k)
+
         out_of = out[C : C + M, :].rearrange("(g p b) n -> g b p n", g=GROUPS, b=BLOCKS)
 
         positions = []
@@ -59,6 +62,12 @@ def tile_autoregressivemodel_kernel(tc, table, row_embed, col_embed, wqkv, bqkv,
             else:
                 nc.gpsimd.tensor_copy(pos_grid, codes[:, k, :].unsqueeze(1).to_broadcast([P, GRID, GRID]))
             positions.append(pos)
+
+        zeros = held.tile([P, BANK], BF16, name="zeros")
+        nc.vector.memset(zeros[:], 0.0)
+        unread = psum.tile([P, BANK], F32, name="acc")
+        for warming in range(WARMING):
+            nc.tensor.matmul(unread[:], zeros[:, 0:P], zeros[:], start=True, stop=True)
 
         h = [held.tile([P, N], F32, name=f"h{k}") for k in range(KB)]
         h_bf16 = [held.tile([P, N], BF16, name=f"h_bf16_{k}") for k in range(KB)]
@@ -76,7 +85,7 @@ def tile_autoregressivemodel_kernel(tc, table, row_embed, col_embed, wqkv, bqkv,
         def project(acc, g, b, j, k):
             nc.tensor.matmul(
                 acc[:],
-                weights_of[g][:, k, b, :],
+                weights[g][k][:].rearrange("c (p b) -> c b p", b=BLOCKS)[:, b, :],
                 h_bf16[k][:, j * BANK : (j + 1) * BANK],
                 start=(k == 0),
                 stop=(k == KB - 1),

@@ -18,7 +18,7 @@ JB = N // BANK
 GROUPS = 3
 BLOCKS = C // P
 assert BLOCKS * JB == BANKS
-WARMING = 16
+WARMING = 12
 
 FLOPS = 2 * C * M * N
 

@@ -18,7 +18,6 @@ JB = N // BANK
 GROUPS = 3
 BLOCKS = C // P
 assert BLOCKS * JB == BANKS
-WARMING = 12
 
 FLOPS = 2 * C * M * N
 
@@ -62,12 +61,6 @@ def tile_autoregressivemodel_kernel(tc, table, row_embed, col_embed, wqkv, bqkv,
             else:
                 nc.gpsimd.tensor_copy(pos_grid, codes[:, k, :].unsqueeze(1).to_broadcast([P, GRID, GRID]))
             positions.append(pos)
-
-        zeros = held.tile([P, BANK], BF16, name="zeros")
-        nc.vector.memset(zeros[:], 0.0)
-        unread = psum.tile([P, BANK], F32, name="acc")
-        for warming in range(WARMING):
-            nc.tensor.matmul(unread[:], zeros[:, 0:P], zeros[:], start=True, stop=True)
 
         h = [held.tile([P, N], F32, name=f"h{k}") for k in range(KB)]
         h_bf16 = [held.tile([P, N], BF16, name=f"h_bf16_{k}") for k in range(KB)]

@@ -19,6 +19,9 @@ GROUPS = 3
 BLOCKS = C // P
 assert BLOCKS * JB == BANKS
 
+WHOLE = [(j * BANK, BANK) for j in range(JB)]
+HALVED = WHOLE[:-1] + [(N - BANK, BANK // 2), (N - BANK // 2, BANK // 2)]
+
 FLOPS = 2 * C * M * N
 
 
@@ -26,7 +29,7 @@ def tile_autoregressivemodel_kernel(tc, table, row_embed, col_embed, wqkv, bqkv,
     nc = tc.nc
     with (
         tc.tile_pool(name="held", bufs=1) as held,
-        tc.tile_pool(name="staging", bufs=GROUPS * BLOCKS * JB) as staging,
+        tc.tile_pool(name="staging", bufs=GROUPS * BLOCKS * JB + 1) as staging,
         tc.psum_pool(name="psum", bufs=BANKS) as psum,
     ):
         codes = held.tile([P, KB, GRID], F32, name="codes")
@@ -65,50 +68,51 @@ def tile_autoregressivemodel_kernel(tc, table, row_embed, col_embed, wqkv, bqkv,
         h = [held.tile([P, N], F32, name=f"h{k}") for k in range(KB)]
         h_bf16 = [held.tile([P, N], BF16, name=f"h_bf16_{k}") for k in range(KB)]
 
-        def embed(k, j):
-            piece = slice(j * BANK, (j + 1) * BANK)
+        def embed(k, first, width):
+            piece = slice(first, first + width)
             nc.vector.tensor_tensor(
                 h[k][:, piece],
-                tables[k][:].indirect(offsets[:, j * (BANK // 16) : (j + 1) * (BANK // 16)]),
+                tables[k][:].indirect(offsets[:, first // 16 : (first + width) // 16]),
                 positions[k][:, piece],
                 ADD,
             )
             nc.scalar.activation(h_bf16[k][:, piece], h[k][:, piece], COPY)
 
-        def project(acc, g, b, j, k):
+        def project(sums, g, b, k, first, width, closes):
             nc.tensor.matmul(
-                acc[:],
+                sums,
                 weights[g][k][:].rearrange("c (p b) -> c b p", b=BLOCKS)[:, b, :],
-                h_bf16[k][:, j * BANK : (j + 1) * BANK],
+                h_bf16[k][:, first : first + width],
                 start=(k == 0),
-                stop=(k == KB - 1),
+                stop=(k == KB - 1 and closes),
             )
 
-        def finish(acc, g, b, j):
-            qkv = staging.tile([P, BANK], F32, name="qkv")
-            if j == 0:
-                nc.scalar.activation(qkv[:], acc[:], IDENTITY, bias=bias[:, g, b : b + 1])
+        def finish(sums, g, b, first, width):
+            qkv = staging.tile([P, width], F32, name="qkv")
+            if first + width == N:
+                nc.vector.tensor_scalar_add(qkv[:], sums, bias[:, g, b : b + 1])
             else:
-                nc.vector.tensor_scalar_add(qkv[:], acc[:], bias[:, g, b : b + 1])
-            nc.sync.dma_start(out_of[g, b, :, j * BANK : (j + 1) * BANK], qkv[:])
+                nc.scalar.activation(qkv[:], sums, IDENTITY, bias=bias[:, g, b : b + 1])
+            nc.sync.dma_start(out_of[g, b, :, first : first + width], qkv[:])
 
         queries = {}
         for k in range(KB):
-            for j in range(JB):
-                embed(k, j)
+            for first, width in HALVED if k == KB - 1 else WHOLE:
+                embed(k, first, width)
+                j, inside = divmod(first, BANK)
                 for b in range(BLOCKS):
                     if k == 0:
                         queries[b, j] = psum.tile([P, BANK], F32, name="acc")
-                    project(queries[b, j], 0, b, j, k)
+                    project(queries[b, j][:, inside : inside + width], 0, b, k, first, width, inside + width == BANK)
             nc.sync.dma_start(out[k * P : (k + 1) * P, :], h[k][:])
-        for j in range(JB):
+        for first, width in WHOLE:
             for b in range(BLOCKS):
-                finish(queries[b, j], 0, b, j)
+                finish(queries[b, first // BANK][:], 0, b, first, width)
 
         for g in range(1, GROUPS):
             for b in range(BLOCKS):
-                for j in range(JB):
-                    acc = psum.tile([P, BANK], F32, name="acc")
+                for first, width in HALVED if (g, b) == (GROUPS - 1, BLOCKS - 1) else WHOLE:
+                    acc = psum.tile([P, width], F32, name="acc")
                     for k in range(KB):
-                        project(acc, g, b, j, k)
-                    finish(acc, g, b, j)
+                        project(acc[:], g, b, k, first, width, True)
+                    finish(acc[:], g, b, first, width)

@@ -19,9 +19,6 @@ GROUPS = 3
 BLOCKS = C // P
 assert BLOCKS * JB == BANKS
 
-WHOLE = [(j * BANK, BANK) for j in range(JB)]
-HALVED = WHOLE[:-1] + [(N - BANK, BANK // 2), (N - BANK // 2, BANK // 2)]
-
 FLOPS = 2 * C * M * N
 
 
@@ -29,7 +26,7 @@ def tile_autoregressivemodel_kernel(tc, table, row_embed, col_embed, wqkv, bqkv,
     nc = tc.nc
     with (
         tc.tile_pool(name="held", bufs=1) as held,
-        tc.tile_pool(name="staging", bufs=GROUPS * BLOCKS * JB + 1) as staging,
+        tc.tile_pool(name="staging", bufs=GROUPS * BLOCKS * JB) as staging,
         tc.psum_pool(name="psum", bufs=BANKS) as psum,
     ):
         codes = held.tile([P, KB, GRID], F32, name="codes")
@@ -65,54 +62,53 @@ def tile_autoregressivemodel_kernel(tc, table, row_embed, col_embed, wqkv, bqkv,
                 nc.gpsimd.tensor_copy(pos_grid, codes[:, k, :].unsqueeze(1).to_broadcast([P, GRID, GRID]))
             positions.append(pos)
 
-        h = [held.tile([P, N], F32, name=f"h{k}") for k in range(KB)]
+        h = held.tile([P, KB, N], F32, name="h")
         h_bf16 = [held.tile([P, N], BF16, name=f"h_bf16_{k}") for k in range(KB)]
 
-        def embed(k, first, width):
-            piece = slice(first, first + width)
+        def embed(k, j):
+            piece = slice(j * BANK, (j + 1) * BANK)
             nc.vector.tensor_tensor(
-                h[k][:, piece],
-                tables[k][:].indirect(offsets[:, first // 16 : (first + width) // 16]),
+                h[:, k, piece],
+                tables[k][:].indirect(offsets[:, j * (BANK // 16) : (j + 1) * (BANK // 16)]),
                 positions[k][:, piece],
                 ADD,
             )
-            nc.scalar.activation(h_bf16[k][:, piece], h[k][:, piece], COPY)
+            nc.scalar.activation(h_bf16[k][:, piece], h[:, k, piece], COPY)
 
-        def project(sums, g, b, k, first, width, closes):
+        def project(acc, g, b, j, k):
             nc.tensor.matmul(
-                sums,
+                acc[:],
                 weights[g][k][:].rearrange("c (p b) -> c b p", b=BLOCKS)[:, b, :],
-                h_bf16[k][:, first : first + width],
+                h_bf16[k][:, j * BANK : (j + 1) * BANK],
                 start=(k == 0),
-                stop=(k == KB - 1 and closes),
+                stop=(k == KB - 1),
             )
 
-        def finish(sums, g, b, first, width):
-            qkv = staging.tile([P, width], F32, name="qkv")
-            if first + width == N:
-                nc.vector.tensor_scalar_add(qkv[:], sums, bias[:, g, b : b + 1])
+        def finish(acc, g, b, j):
+            qkv = staging.tile([P, BANK], F32, name="qkv")
+            if j == 0:
+                nc.scalar.activation(qkv[:], acc[:], IDENTITY, bias=bias[:, g, b : b + 1])
             else:
-                nc.scalar.activation(qkv[:], sums, IDENTITY, bias=bias[:, g, b : b + 1])
-            nc.sync.dma_start(out_of[g, b, :, first : first + width], qkv[:])
+                nc.vector.tensor_scalar_add(qkv[:], acc[:], bias[:, g, b : b + 1])
+            nc.sync.dma_start(out_of[g, b, :, j * BANK : (j + 1) * BANK], qkv[:])
 
         queries = {}
         for k in range(KB):
-            for first, width in HALVED if k == KB - 1 else WHOLE:
-                embed(k, first, width)
-                j, inside = divmod(first, BANK)
+            for j in range(JB):
+                embed(k, j)
                 for b in range(BLOCKS):
                     if k == 0:
                         queries[b, j] = psum.tile([P, BANK], F32, name="acc")
-                    project(queries[b, j][:, inside : inside + width], 0, b, k, first, width, inside + width == BANK)
-            nc.sync.dma_start(out[k * P : (k + 1) * P, :], h[k][:])
-        for first, width in WHOLE:
+                    project(queries[b, j], 0, b, j, k)
+        nc.sync.dma_start(out[0:C, :].rearrange("(k p) n -> p k n", p=P), h[:])
+        for j in range(JB):
             for b in range(BLOCKS):
-                finish(queries[b, first // BANK][:], 0, b, first, width)
+                finish(queries[b, j], 0, b, j)
 
         for g in range(1, GROUPS):
             for b in range(BLOCKS):
-                for first, width in HALVED if (g, b) == (GROUPS - 1, BLOCKS - 1) else WHOLE:
-                    acc = psum.tile([P, width], F32, name="acc")
+                for j in range(JB):
+                    acc = psum.tile([P, BANK], F32, name="acc")
                     for k in range(KB):
-                        project(acc[:], g, b, k, first, width, True)
-                    finish(acc[:], g, b, first, width)
+                        project(acc, g, b, j, k)
+                    finish(acc, g, b, j)

@@ -13,6 +13,7 @@ GRID = 32
 N = GRID * GRID
 BANK = 512
 BANKS = 8
+SHORT = 128
 KB = C // P
 JB = N // BANK
 GROUPS = 3
@@ -65,22 +66,22 @@ def tile_autoregressivemodel_kernel(tc, table, row_embed, col_embed, wqkv, bqkv,
         h = held.tile([P, KB, N], F32, name="h")
         h_bf16 = [held.tile([P, N], BF16, name=f"h_bf16_{k}") for k in range(KB)]
 
-        def embed(k, j):
-            piece = slice(j * BANK, (j + 1) * BANK)
+        def embed(k, first, width):
+            tokens = slice(first, first + width)
             nc.vector.tensor_tensor(
-                h[:, k, piece],
-                tables[k][:].indirect(offsets[:, j * (BANK // 16) : (j + 1) * (BANK // 16)]),
-                positions[k][:, piece],
+                h[:, k, tokens],
+                tables[k][:].indirect(offsets[:, first // 16 : (first + width) // 16]),
+                positions[k][:, tokens],
                 ADD,
             )
-            nc.scalar.activation(h_bf16[k][:, piece], h[:, k, piece], COPY)
+            nc.scalar.activation(h_bf16[k][:, tokens], h[:, k, tokens], COPY)
 
-        def project(acc, g, b, j, k):
+        def project(acc, g, b, k, first, width, start):
             nc.tensor.matmul(
-                acc[:],
+                acc,
                 weights[g][k][:].rearrange("c (p b) -> c b p", b=BLOCKS)[:, b, :],
-                h_bf16[k][:, j * BANK : (j + 1) * BANK],
-                start=(k == 0),
+                h_bf16[k][:, first : first + width],
+                start=start,
                 stop=(k == KB - 1),
             )
 
@@ -92,23 +93,25 @@ def tile_autoregressivemodel_kernel(tc, table, row_embed, col_embed, wqkv, bqkv,
                 nc.vector.tensor_scalar_add(qkv[:], acc[:], bias[:, g, b : b + 1])
             nc.sync.dma_start(out_of[g, b, :, j * BANK : (j + 1) * BANK], qkv[:])
 
-        queries = {}
+        queries = [[psum.tile([P, BANK], F32, name="acc") for b in range(BLOCKS)] for j in range(JB)]
         for k in range(KB):
-            for j in range(JB):
-                embed(k, j)
+            first = 0
+            while first < N:
+                width = BANK if k > 0 else max(first, SHORT)
+                embed(k, first, width)
+                j, column = divmod(first, BANK)
                 for b in range(BLOCKS):
-                    if k == 0:
-                        queries[b, j] = psum.tile([P, BANK], F32, name="acc")
-                    project(queries[b, j], 0, b, j, k)
+                    project(queries[j][b][:, column : column + width], 0, b, k, first, width, start=(k == 0 and column == 0))
+                first += width
         nc.sync.dma_start(out[0:C, :].rearrange("(k p) n -> p k n", p=P), h[:])
         for j in range(JB):
             for b in range(BLOCKS):
-                finish(queries[b, j], 0, b, j)
+                finish(queries[j][b], 0, b, j)
 
         for g in range(1, GROUPS):
             for b in range(BLOCKS):
                 for j in range(JB):
                     acc = psum.tile([P, BANK], F32, name="acc")
                     for k in range(KB):
-                        project(acc, g, b, j, k)
+                        project(acc[:], g, b, k, j * BANK, BANK, start=(k == 0))
                     finish(acc, g, b, j)

@@ -14,6 +14,7 @@ N = GRID * GRID
 BANK = 512
 BANKS = 8
 SHORT = 128
+HALF = BANK // 2
 KB = C // P
 JB = N // BANK
 GROUPS = 3
@@ -27,7 +28,7 @@ def tile_autoregressivemodel_kernel(tc, table, row_embed, col_embed, wqkv, bqkv,
     nc = tc.nc
     with (
         tc.tile_pool(name="held", bufs=1) as held,
-        tc.tile_pool(name="staging", bufs=GROUPS * BLOCKS * JB) as staging,
+        tc.tile_pool(name="staging", bufs=GROUPS * BLOCKS * JB + 1) as staging,
         tc.psum_pool(name="psum", bufs=BANKS) as psum,
     ):
         codes = held.tile([P, KB, GRID], F32, name="codes")
@@ -39,17 +40,18 @@ def tile_autoregressivemodel_kernel(tc, table, row_embed, col_embed, wqkv, bqkv,
         offsets = held.tile([P, N // 16], U16, name="offsets")
         nc.sync.dma_start(offsets[:], offs)
         tables = [held.tile([P, S], F32, name=f"table{k}") for k in range(KB)]
-        weights = [[held.tile([P, C], BF16, name=f"weights{g}_{k}") for k in range(KB)] for g in range(GROUPS)]
-
-        def load_weights(g, k):
-            nc.sync.dma_start(weights[g][k][:], wqkv[k * P : (k + 1) * P, g * C : (g + 1) * C])
+        weights_q = [held.tile([P, C], BF16, name=f"weights_q{k}") for k in range(KB)]
+        weights_kv = [held.tile([P, M - C], BF16, name=f"weights_kv{k}") for k in range(KB)]
 
         for k in range(KB):
             nc.sync.dma_start(tables[k][:], table[k * P : (k + 1) * P, :])
-            load_weights(0, k)
-        for g in range(1, GROUPS):
-            for k in range(KB):
-                load_weights(g, k)
+            nc.sync.dma_start(weights_q[k][:], wqkv[k * P : (k + 1) * P, 0:C])
+        for k in range(KB):
+            nc.sync.dma_start(weights_kv[k][:], wqkv[k * P : (k + 1) * P, C:M])
+
+        def stationary(g, b, k):
+            group = weights_q[k][:] if g == 0 else weights_kv[k][:, (g - 1) * C : g * C]
+            return group.rearrange("c (p b) -> c b p", b=BLOCKS)[:, b, :]
 
         out_of = out[C : C + M, :].rearrange("(g p b) n -> g b p n", g=GROUPS, b=BLOCKS)
 
@@ -76,42 +78,47 @@ def tile_autoregressivemodel_kernel(tc, table, row_embed, col_embed, wqkv, bqkv,
             )
             nc.scalar.activation(h_bf16[k][:, tokens], h[:, k, tokens], COPY)
 
-        def project(acc, g, b, k, first, width, start):
+        def project(acc, g, b, k, first, width, start, stop):
             nc.tensor.matmul(
                 acc,
-                weights[g][k][:].rearrange("c (p b) -> c b p", b=BLOCKS)[:, b, :],
+                stationary(g, b, k),
                 h_bf16[k][:, first : first + width],
                 start=start,
-                stop=(k == KB - 1),
+                stop=stop,
             )
 
-        def finish(acc, g, b, j):
-            qkv = staging.tile([P, BANK], F32, name="qkv")
-            if j == 0:
+        def finish(acc, g, b, first, width):
+            qkv = staging.tile([P, width], F32, name="qkv")
+            if first < BANK:
                 nc.scalar.activation(qkv[:], acc[:], IDENTITY, bias=bias[:, g, b : b + 1])
             else:
                 nc.vector.tensor_scalar_add(qkv[:], acc[:], bias[:, g, b : b + 1])
-            nc.sync.dma_start(out_of[g, b, :, j * BANK : (j + 1) * BANK], qkv[:])
+            nc.sync.dma_start(out_of[g, b, :, first : first + width], qkv[:])
 
         queries = [[psum.tile([P, BANK], F32, name="acc") for b in range(BLOCKS)] for j in range(JB)]
         for k in range(KB):
             first = 0
             while first < N:
-                width = BANK if k > 0 else max(first, SHORT)
+                width = max(first, SHORT) if k == 0 else HALF if k == KB - 1 else BANK
                 embed(k, first, width)
                 j, column = divmod(first, BANK)
                 for b in range(BLOCKS):
-                    project(queries[j][b][:, column : column + width], 0, b, k, first, width, start=(k == 0 and column == 0))
+                    project(
+                        queries[j][b][:, column : column + width], 0, b, k, first, width,
+                        start=(k == 0 and column == 0), stop=(k == KB - 1 and column + width == BANK),
+                    )
                 first += width
         nc.sync.dma_start(out[0:C, :].rearrange("(k p) n -> p k n", p=P), h[:])
         for j in range(JB):
             for b in range(BLOCKS):
-                finish(queries[j][b], 0, b, j)
+                finish(queries[j][b], 0, b, j * BANK, BANK)
 
         for g in range(1, GROUPS):
             for b in range(BLOCKS):
                 for j in range(JB):
-                    acc = psum.tile([P, BANK], F32, name="acc")
-                    for k in range(KB):
-                        project(acc[:], g, b, k, j * BANK, BANK, start=(k == 0))
-                    finish(acc, g, b, j)
+                    width = HALF if (g, b, j) == (GROUPS - 1, BLOCKS - 1, JB - 1) else BANK
+                    for first in range(j * BANK, (j + 1) * BANK, width):
+                        acc = psum.tile([P, width], F32, name="acc")
+                        for k in range(KB):
+                            project(acc[:], g, b, k, first, width, start=(k == 0), stop=(k == KB - 1))
+                        finish(acc, g, b, first, width)

@@ -17,9 +17,12 @@ SHORT = 128
 HALF = BANK // 2
 KB = C // P
 JB = N // BANK
-GROUPS = 3
-BLOCKS = C // P
-assert BLOCKS * JB == BANKS
+
+EARLY, LATE = 5, 7
+GROUP_BLOCKS = (EARLY, LATE)
+GROUP_ROW = (0, EARLY * P)
+PARKED = EARLY * JB - BANKS
+assert (EARLY + LATE) * P == M
 
 FLOPS = 2 * C * M * N
 
@@ -28,32 +31,39 @@ def tile_autoregressivemodel_kernel(tc, table, row_embed, col_embed, wqkv, bqkv,
     nc = tc.nc
     with (
         tc.tile_pool(name="held", bufs=1) as held,
-        tc.tile_pool(name="staging", bufs=GROUPS * BLOCKS * JB + 1) as staging,
+        tc.tile_pool(name="staging", bufs=(EARLY + LATE) * JB + 1) as staging,
         tc.psum_pool(name="psum", bufs=BANKS) as psum,
     ):
         codes = held.tile([P, KB, GRID], F32, name="codes")
         nc.scalar.dma_start(codes[:, 0 : KB // 2, :], row_embed.rearrange("(k p) g -> p k g", p=P))
         nc.scalar.dma_start(codes[:, KB // 2 : KB, :], col_embed.rearrange("(k p) g -> p k g", p=P))
-        bias = held.tile([P, GROUPS, BLOCKS], F32, name="bias")
-        nc.scalar.dma_start(bias[:], bqkv.rearrange("(g p b) o -> p g (b o)", g=GROUPS, b=BLOCKS))
+        biases = []
+        for g, blocks in enumerate(GROUP_BLOCKS):
+            bias = held.tile([P, blocks], F32, name=f"bias{g}")
+            rows = bqkv[GROUP_ROW[g] : GROUP_ROW[g] + blocks * P, :]
+            nc.scalar.dma_start(bias[:], rows.rearrange("(p b) o -> p (b o)", b=blocks))
+            biases.append(bias)
 
         offsets = held.tile([P, N // 16], U16, name="offsets")
         nc.sync.dma_start(offsets[:], offs)
         tables = [held.tile([P, S], F32, name=f"table{k}") for k in range(KB)]
-        weights_q = [held.tile([P, C], BF16, name=f"weights_q{k}") for k in range(KB)]
-        weights_kv = [held.tile([P, M - C], BF16, name=f"weights_kv{k}") for k in range(KB)]
-
+        weights = [
+            [held.tile([P, blocks * P], BF16, name=f"weights{g}_{k}") for k in range(KB)]
+            for g, blocks in enumerate(GROUP_BLOCKS)
+        ]
         for k in range(KB):
             nc.sync.dma_start(tables[k][:], table[k * P : (k + 1) * P, :])
-            nc.sync.dma_start(weights_q[k][:], wqkv[k * P : (k + 1) * P, 0:C])
+            nc.sync.dma_start(weights[0][k][:], wqkv[k * P : (k + 1) * P, 0 : EARLY * P])
         for k in range(KB):
-            nc.sync.dma_start(weights_kv[k][:], wqkv[k * P : (k + 1) * P, C:M])
+            nc.sync.dma_start(weights[1][k][:], wqkv[k * P : (k + 1) * P, EARLY * P : M])
 
         def stationary(g, b, k):
-            group = weights_q[k][:] if g == 0 else weights_kv[k][:, (g - 1) * C : g * C]
-            return group.rearrange("c (p b) -> c b p", b=BLOCKS)[:, b, :]
+            return weights[g][k][:].rearrange("c (p b) -> c b p", b=GROUP_BLOCKS[g])[:, b, :]
 
-        out_of = out[C : C + M, :].rearrange("(g p b) n -> g b p n", g=GROUPS, b=BLOCKS)
+        def rows_of(g, b):
+            first_row = C + GROUP_ROW[g]
+            group = out[first_row : first_row + GROUP_BLOCKS[g] * P, :]
+            return group.rearrange("(p b) n -> b p n", b=GROUP_BLOCKS[g])[b, :, :]
 
         positions = []
         for k in range(KB):
@@ -87,38 +97,63 @@ def tile_autoregressivemodel_kernel(tc, table, row_embed, col_embed, wqkv, bqkv,
                 stop=stop,
             )
 
+        def add_bias(result, acc, g, b, on_scalar):
+            if on_scalar:
+                nc.scalar.activation(result[:], acc[:], IDENTITY, bias=biases[g][:, b : b + 1])
+            else:
+                nc.vector.tensor_scalar_add(result[:], acc[:], biases[g][:, b : b + 1])
+
         def finish(acc, g, b, first, width):
             qkv = staging.tile([P, width], F32, name="qkv")
-            if first < BANK:
-                nc.scalar.activation(qkv[:], acc[:], IDENTITY, bias=bias[:, g, b : b + 1])
-            else:
-                nc.vector.tensor_scalar_add(qkv[:], acc[:], bias[:, g, b : b + 1])
-            nc.sync.dma_start(out_of[g, b, :, first : first + width], qkv[:])
+            add_bias(qkv, acc, g, b, on_scalar=(b + first // BANK) % 2 == 0)
+            nc.sync.dma_start(rows_of(g, b)[:, first : first + width], qkv[:])
 
-        queries = [[psum.tile([P, BANK], F32, name="acc") for b in range(BLOCKS)] for j in range(JB)]
+        early = [(j, b) for j in range(JB) for b in range(EARLY)]
+        parked_sums, waiting_sums = early[:PARKED], early[BANKS:]
+        accs = {}
+        for j, b in early[:BANKS]:
+            accs[j, b] = psum.tile([P, BANK], F32, name="acc")
+        parked = {}
         for k in range(KB):
+            last = k == KB - 1
             first = 0
             while first < N:
-                width = max(first, SHORT) if k == 0 else HALF if k == KB - 1 else BANK
+                width = max(first, SHORT) if k == 0 else HALF if last else BANK
                 embed(k, first, width)
                 j, column = divmod(first, BANK)
-                for b in range(BLOCKS):
-                    project(
-                        queries[j][b][:, column : column + width], 0, b, k, first, width,
-                        start=(k == 0 and column == 0), stop=(k == KB - 1 and column + width == BANK),
-                    )
+                for b in range(EARLY):
+                    if (j, b) in accs:
+                        closes = last or (k == KB - 2 and (j, b) in parked_sums)
+                        project(
+                            accs[j, b][:, column : column + width], 0, b, k, first, width,
+                            start=(k == 0 and column == 0), stop=(closes and column + width == BANK),
+                        )
                 first += width
-        nc.sync.dma_start(out[0:C, :].rearrange("(k p) n -> p k n", p=P), h[:])
-        for j in range(JB):
-            for b in range(BLOCKS):
-                finish(queries[j][b], 0, b, j * BANK, BANK)
+            if k == KB - 2:
+                for j, b in parked_sums:
+                    parked[j, b] = held.tile([P, BANK], F32, name=f"parked{j}_{b}")
+                    add_bias(parked[j, b], accs.pop((j, b)), 0, b, on_scalar=True)
+                for j, b in waiting_sums:
+                    acc = psum.tile([P, BANK], F32, name="acc")
+                    for i in range(k + 1):
+                        project(acc[:], 0, b, i, j * BANK, BANK, start=(i == 0), stop=False)
+                    accs[j, b] = acc
 
-        for g in range(1, GROUPS):
-            for b in range(BLOCKS):
-                for j in range(JB):
-                    width = HALF if (g, b, j) == (GROUPS - 1, BLOCKS - 1, JB - 1) else BANK
-                    for first in range(j * BANK, (j + 1) * BANK, width):
-                        acc = psum.tile([P, width], F32, name="acc")
-                        for k in range(KB):
-                            project(acc[:], g, b, k, first, width, start=(k == 0), stop=(k == KB - 1))
-                        finish(acc, g, b, first, width)
+        nc.sync.dma_start(out[0:C, :].rearrange("(k p) n -> p k n", p=P), h[:])
+        for j, b in early[PARKED:]:
+            finish(accs[j, b], 0, b, j * BANK, BANK)
+        for j, b in parked_sums:
+            acc = psum.tile([P, BANK], F32, name="acc")
+            project(acc[:], 0, b, KB - 1, j * BANK, BANK, start=True, stop=True)
+            qkv = staging.tile([P, BANK], F32, name="qkv")
+            nc.vector.tensor_tensor(qkv[:], acc[:], parked[j, b][:], ADD)
+            nc.sync.dma_start(rows_of(0, b)[:, j * BANK : (j + 1) * BANK], qkv[:])
+
+        for b in range(LATE):
+            for j in range(JB):
+                width = HALF if (b, j) == (LATE - 1, JB - 1) else BANK
+                for first in range(j * BANK, (j + 1) * BANK, width):
+                    acc = psum.tile([P, width], F32, name="acc")
+                    for k in range(KB):
+                        project(acc[:], 1, b, k, first, width, start=(k == 0), stop=(k == KB - 1))
+                    finish(acc, 1, b, first, width)

@@ -129,6 +129,9 @@ def tile_autoregressivemodel_kernel(tc, table, row_embed, col_embed, wqkv, bqkv,
                             start=(k == 0 and column == 0), stop=(closes and column + width == BANK),
                         )
                 first += width
+            if k % 2 == 1:
+                pair = out[(k - 1) * P : (k + 1) * P, :]
+                nc.sync.dma_start(pair.rearrange("(k p) n -> p k n", p=P), h[:, k - 1 : k + 1, :])
             if k == KB - 2:
                 for j, b in parked_sums:
                     parked[j, b] = held.tile([P, BANK], F32, name=f"parked{j}_{b}")
@@ -139,7 +142,6 @@ def tile_autoregressivemodel_kernel(tc, table, row_embed, col_embed, wqkv, bqkv,
                         project(acc[:], 0, b, i, j * BANK, BANK, start=(i == 0), stop=False)
                     accs[j, b] = acc
 
-        nc.sync.dma_start(out[0:C, :].rearrange("(k p) n -> p k n", p=P), h[:])
         for j, b in early[PARKED:]:
             finish(accs[j, b], 0, b, j * BANK, BANK)
         for j, b in parked_sums:

@@ -118,7 +118,7 @@ def tile_autoregressivemodel_kernel(tc, table, row_embed, col_embed, wqkv, bqkv,
             last = k == KB - 1
             first = 0
             while first < N:
-                width = max(first, SHORT) if k == 0 else HALF if last else BANK
+                width = max(first, SHORT) if k == 0 else BANK if last else HALF
                 embed(k, first, width)
                 j, column = divmod(first, BANK)
                 for b in range(EARLY):

@@ -129,9 +129,7 @@ def tile_autoregressivemodel_kernel(tc, table, row_embed, col_embed, wqkv, bqkv,
                             start=(k == 0 and column == 0), stop=(closes and column + width == BANK),
                         )
                 first += width
-            if k % 2 == 1:
-                pair = out[(k - 1) * P : (k + 1) * P, :]
-                nc.sync.dma_start(pair.rearrange("(k p) n -> p k n", p=P), h[:, k - 1 : k + 1, :])
+            nc.sync.dma_start(out[k * P : (k + 1) * P, :], h[:, k, :])
             if k == KB - 2:
                 for j, b in parked_sums:
                     parked[j, b] = held.tile([P, BANK], F32, name=f"parked{j}_{b}")

@@ -118,7 +118,7 @@ def tile_autoregressivemodel_kernel(tc, table, row_embed, col_embed, wqkv, bqkv,
             last = k == KB - 1
             first = 0
             while first < N:
-                width = max(first, SHORT) if k == 0 else BANK if last else HALF
+                width = max(first, SHORT) if k == 0 else HALF
                 embed(k, first, width)
                 j, column = divmod(first, BANK)
                 for b in range(EARLY):

@@ -18,10 +18,11 @@ HALF = BANK // 2
 KB = C // P
 JB = N // BANK
 
-EARLY, LATE = 5, 7
+EARLY, LATE = 6, 6
 GROUP_BLOCKS = (EARLY, LATE)
 GROUP_ROW = (0, EARLY * P)
-PARKED = EARLY * JB - BANKS
+LENT = 2
+assert (KB - 2) * LENT == EARLY * JB - BANKS
 assert (EARLY + LATE) * P == M
 
 FLOPS = 2 * C * M * N
@@ -97,56 +98,56 @@ def tile_autoregressivemodel_kernel(tc, table, row_embed, col_embed, wqkv, bqkv,
                 stop=stop,
             )
 
-        def add_bias(result, acc, g, b, on_scalar):
-            if on_scalar:
-                nc.scalar.activation(result[:], acc[:], IDENTITY, bias=biases[g][:, b : b + 1])
-            else:
-                nc.vector.tensor_scalar_add(result[:], acc[:], biases[g][:, b : b + 1])
-
         def finish(acc, g, b, first, width):
             qkv = staging.tile([P, width], F32, name="qkv")
-            add_bias(qkv, acc, g, b, on_scalar=(b + first // BANK) % 2 == 0)
+            bias = biases[g][:, b : b + 1]
+            if (b + first // BANK) % 2 == 0:
+                nc.scalar.activation(qkv[:], acc[:], IDENTITY, bias=bias)
+            else:
+                nc.vector.tensor_scalar_add(qkv[:], acc[:], bias)
             nc.sync.dma_start(rows_of(g, b)[:, first : first + width], qkv[:])
 
         early = [(j, b) for j in range(JB) for b in range(EARLY)]
-        parked_sums, waiting_sums = early[:PARKED], early[BANKS:]
-        accs = {}
+        sums = {}
         for j, b in early[:BANKS]:
-            accs[j, b] = psum.tile([P, BANK], F32, name="acc")
-        parked = {}
+            sums[j, b] = psum.tile([P, BANK], F32, name="acc")
+        waiting = early[BANKS:]
+        parked = []
         for k in range(KB):
             last = k == KB - 1
+            leaving = [] if k == 0 or last else early[(k - 1) * LENT : k * LENT]
             first = 0
             while first < N:
                 width = max(first, SHORT) if k == 0 else HALF
                 embed(k, first, width)
                 j, column = divmod(first, BANK)
                 for b in range(EARLY):
-                    if (j, b) in accs:
-                        closes = last or (k == KB - 2 and (j, b) in parked_sums)
+                    if (j, b) in sums:
+                        closes = (last or (j, b) in leaving) and column + width == BANK
                         project(
-                            accs[j, b][:, column : column + width], 0, b, k, first, width,
-                            start=(k == 0 and column == 0), stop=(closes and column + width == BANK),
+                            sums[j, b][:, column : column + width], 0, b, k, first, width,
+                            start=(k == 0 and column == 0), stop=closes,
                         )
                 first += width
             nc.sync.dma_start(out[k * P : (k + 1) * P, :], h[:, k, :])
-            if k == KB - 2:
-                for j, b in parked_sums:
-                    parked[j, b] = held.tile([P, BANK], F32, name=f"parked{j}_{b}")
-                    add_bias(parked[j, b], accs.pop((j, b)), 0, b, on_scalar=True)
-                for j, b in waiting_sums:
-                    acc = psum.tile([P, BANK], F32, name="acc")
-                    for i in range(k + 1):
-                        project(acc[:], 0, b, i, j * BANK, BANK, start=(i == 0), stop=False)
-                    accs[j, b] = acc
+            for j, b in leaving:
+                part = held.tile([P, BANK], F32, name=f"part{j}_{b}")
+                nc.scalar.activation(part[:], sums.pop((j, b))[:], IDENTITY, bias=biases[0][:, b : b + 1])
+                parked.append((part, j, b, k + 1))
+                j_next, b_next = waiting.pop(0)
+                acc = psum.tile([P, BANK], F32, name="acc")
+                for i in range(k + 1):
+                    project(acc[:], 0, b_next, i, j_next * BANK, BANK, start=(i == 0), stop=False)
+                sums[j_next, b_next] = acc
 
-        for j, b in early[PARKED:]:
-            finish(accs[j, b], 0, b, j * BANK, BANK)
-        for j, b in parked_sums:
+        for j, b in sums:
+            finish(sums[j, b], 0, b, j * BANK, BANK)
+        for part, j, b, first_missing in parked:
             acc = psum.tile([P, BANK], F32, name="acc")
-            project(acc[:], 0, b, KB - 1, j * BANK, BANK, start=True, stop=True)
+            for k in range(first_missing, KB):
+                project(acc[:], 0, b, k, j * BANK, BANK, start=(k == first_missing), stop=(k == KB - 1))
             qkv = staging.tile([P, BANK], F32, name="qkv")
-            nc.vector.tensor_tensor(qkv[:], acc[:], parked[j, b][:], ADD)
+            nc.vector.tensor_tensor(qkv[:], acc[:], part[:], ADD)
             nc.sync.dma_start(rows_of(0, b)[:, j * BANK : (j + 1) * BANK], qkv[:])
 
         for b in range(LATE):

@@ -118,7 +118,7 @@ def tile_autoregressivemodel_kernel(tc, table, row_embed, col_embed, wqkv, bqkv,
             leaving = [] if k == 0 or last else early[(k - 1) * LENT : k * LENT]
             first = 0
             while first < N:
-                width = max(first, SHORT) if k == 0 else HALF
+                width = max(first, SHORT) if k == 0 else HALF if k == 1 else BANK
                 embed(k, first, width)
                 j, column = divmod(first, BANK)
                 for b in range(EARLY):
@@ -152,9 +152,12 @@ def tile_autoregressivemodel_kernel(tc, table, row_embed, col_embed, wqkv, bqkv,
 
         for b in range(LATE):
             for j in range(JB):
-                width = HALF if (b, j) == (LATE - 1, JB - 1) else BANK
-                for first in range(j * BANK, (j + 1) * BANK, width):
+                final = (b, j) == (LATE - 1, JB - 1)
+                first, end = j * BANK, (j + 1) * BANK
+                while first < end:
+                    width = max((end - first) // 2, SHORT) if final else BANK
                     acc = psum.tile([P, width], F32, name="acc")
                     for k in range(KB):
                         project(acc[:], 1, b, k, first, width, start=(k == 0), stop=(k == KB - 1))
                     finish(acc, 1, b, first, width)
+                    first += width

@@ -18,12 +18,12 @@ HALF = BANK // 2
 KB = C // P
 JB = N // BANK
 
-EARLY, LATE = 6, 6
-GROUP_BLOCKS = (EARLY, LATE)
-GROUP_ROW = (0, EARLY * P)
+EARLY, LATE = 0, 1
+GROUPS = 2
+ROWS = M // GROUPS
+BLOCKS = ROWS // P
 LENT = 2
-assert (KB - 2) * LENT == EARLY * JB - BANKS
-assert (EARLY + LATE) * P == M
+assert (KB - 2) * LENT == BLOCKS * JB - BANKS
 
 FLOPS = 2 * C * M * N
 
@@ -32,39 +32,29 @@ def tile_autoregressivemodel_kernel(tc, table, row_embed, col_embed, wqkv, bqkv,
     nc = tc.nc
     with (
         tc.tile_pool(name="held", bufs=1) as held,
-        tc.tile_pool(name="staging", bufs=(EARLY + LATE) * JB + 1) as staging,
+        tc.tile_pool(name="staging", bufs=GROUPS * BLOCKS * JB + 2) as staging,
         tc.psum_pool(name="psum", bufs=BANKS) as psum,
     ):
         codes = held.tile([P, KB, GRID], F32, name="codes")
         nc.scalar.dma_start(codes[:, 0 : KB // 2, :], row_embed.rearrange("(k p) g -> p k g", p=P))
         nc.scalar.dma_start(codes[:, KB // 2 : KB, :], col_embed.rearrange("(k p) g -> p k g", p=P))
-        biases = []
-        for g, blocks in enumerate(GROUP_BLOCKS):
-            bias = held.tile([P, blocks], F32, name=f"bias{g}")
-            rows = bqkv[GROUP_ROW[g] : GROUP_ROW[g] + blocks * P, :]
-            nc.scalar.dma_start(bias[:], rows.rearrange("(p b) o -> p (b o)", b=blocks))
-            biases.append(bias)
 
         offsets = held.tile([P, N // 16], U16, name="offsets")
         nc.sync.dma_start(offsets[:], offs)
         tables = [held.tile([P, S], F32, name=f"table{k}") for k in range(KB)]
-        weights = [
-            [held.tile([P, blocks * P], BF16, name=f"weights{g}_{k}") for k in range(KB)]
-            for g, blocks in enumerate(GROUP_BLOCKS)
-        ]
+        weights = [[held.tile([P, ROWS], BF16, name=f"weights{g}_{k}") for k in range(KB)] for g in range(GROUPS)]
         for k in range(KB):
             nc.sync.dma_start(tables[k][:], table[k * P : (k + 1) * P, :])
-            nc.sync.dma_start(weights[0][k][:], wqkv[k * P : (k + 1) * P, 0 : EARLY * P])
+            nc.sync.dma_start(weights[EARLY][k][:], wqkv[k * P : (k + 1) * P, 0:ROWS])
+        bias = held.tile([P, GROUPS, BLOCKS], F32, name="bias")
+        nc.sync.dma_start(bias[:], bqkv.rearrange("(g p b) o -> p g (b o)", g=GROUPS, b=BLOCKS))
         for k in range(KB):
-            nc.sync.dma_start(weights[1][k][:], wqkv[k * P : (k + 1) * P, EARLY * P : M])
+            nc.sync.dma_start(weights[LATE][k][:], wqkv[k * P : (k + 1) * P, ROWS:M])
 
         def stationary(g, b, k):
-            return weights[g][k][:].rearrange("c (p b) -> c b p", b=GROUP_BLOCKS[g])[:, b, :]
+            return weights[g][k][:].rearrange("c (p b) -> c b p", b=BLOCKS)[:, b, :]
 
-        def rows_of(g, b):
-            first_row = C + GROUP_ROW[g]
-            group = out[first_row : first_row + GROUP_BLOCKS[g] * P, :]
-            return group.rearrange("(p b) n -> b p n", b=GROUP_BLOCKS[g])[b, :, :]
+        out_of = out[C : C + M, :].rearrange("(g p b) n -> g b p n", g=GROUPS, b=BLOCKS)
 
         positions = []
         for k in range(KB):
@@ -100,14 +90,14 @@ def tile_autoregressivemodel_kernel(tc, table, row_embed, col_embed, wqkv, bqkv,
 
         def finish(acc, g, b, first, width):
             qkv = staging.tile([P, width], F32, name="qkv")
-            bias = biases[g][:, b : b + 1]
+            bias_b = bias[:, g, b : b + 1]
             if (b + first // BANK) % 2 == 0:
-                nc.scalar.activation(qkv[:], acc[:], IDENTITY, bias=bias)
+                nc.scalar.activation(qkv[:], acc[:], IDENTITY, bias=bias_b)
             else:
-                nc.vector.tensor_scalar_add(qkv[:], acc[:], bias)
-            nc.sync.dma_start(rows_of(g, b)[:, first : first + width], qkv[:])
+                nc.vector.tensor_scalar_add(qkv[:], acc[:], bias_b)
+            nc.sync.dma_start(out_of[g, b, :, first : first + width], qkv[:])
 
-        early = [(j, b) for j in range(JB) for b in range(EARLY)]
+        early = [(j, b) for j in range(JB) for b in range(BLOCKS)]
         sums = {}
         for j, b in early[:BANKS]:
             sums[j, b] = psum.tile([P, BANK], F32, name="acc")
@@ -121,43 +111,43 @@ def tile_autoregressivemodel_kernel(tc, table, row_embed, col_embed, wqkv, bqkv,
                 width = max(first, SHORT) if k == 0 else HALF if k == 1 else BANK
                 embed(k, first, width)
                 j, column = divmod(first, BANK)
-                for b in range(EARLY):
+                for b in range(BLOCKS):
                     if (j, b) in sums:
                         closes = (last or (j, b) in leaving) and column + width == BANK
                         project(
-                            sums[j, b][:, column : column + width], 0, b, k, first, width,
+                            sums[j, b][:, column : column + width], EARLY, b, k, first, width,
                             start=(k == 0 and column == 0), stop=closes,
                         )
                 first += width
             nc.sync.dma_start(out[k * P : (k + 1) * P, :], h[:, k, :])
             for j, b in leaving:
                 part = held.tile([P, BANK], F32, name=f"part{j}_{b}")
-                nc.scalar.activation(part[:], sums.pop((j, b))[:], IDENTITY, bias=biases[0][:, b : b + 1])
+                nc.scalar.activation(part[:], sums.pop((j, b))[:], COPY)
                 parked.append((part, j, b, k + 1))
                 j_next, b_next = waiting.pop(0)
                 acc = psum.tile([P, BANK], F32, name="acc")
                 for i in range(k + 1):
-                    project(acc[:], 0, b_next, i, j_next * BANK, BANK, start=(i == 0), stop=False)
+                    project(acc[:], EARLY, b_next, i, j_next * BANK, BANK, start=(i == 0), stop=False)
                 sums[j_next, b_next] = acc
 
         for j, b in sums:
-            finish(sums[j, b], 0, b, j * BANK, BANK)
+            finish(sums[j, b], EARLY, b, j * BANK, BANK)
         for part, j, b, first_missing in parked:
             acc = psum.tile([P, BANK], F32, name="acc")
             for k in range(first_missing, KB):
-                project(acc[:], 0, b, k, j * BANK, BANK, start=(k == first_missing), stop=(k == KB - 1))
+                project(acc[:], EARLY, b, k, j * BANK, BANK, start=(k == first_missing), stop=(k == KB - 1))
             qkv = staging.tile([P, BANK], F32, name="qkv")
-            nc.vector.tensor_tensor(qkv[:], acc[:], part[:], ADD)
-            nc.sync.dma_start(rows_of(0, b)[:, j * BANK : (j + 1) * BANK], qkv[:])
+            nc.vector.scalar_tensor_tensor(qkv[:], acc[:], bias[:, EARLY, b : b + 1], part[:], ADD, ADD)
+            nc.sync.dma_start(out_of[EARLY, b, :, j * BANK : (j + 1) * BANK], qkv[:])
 
-        for b in range(LATE):
+        for b in range(BLOCKS):
             for j in range(JB):
-                final = (b, j) == (LATE - 1, JB - 1)
+                final = (b, j) == (BLOCKS - 1, JB - 1)
                 first, end = j * BANK, (j + 1) * BANK
                 while first < end:
                     width = max((end - first) // 2, SHORT) if final else BANK
                     acc = psum.tile([P, width], F32, name="acc")
                     for k in range(KB):
-                        project(acc[:], 1, b, k, first, width, start=(k == 0), stop=(k == KB - 1))
-                    finish(acc, 1, b, first, width)
+                        project(acc[:], LATE, b, k, first, width, start=(k == 0), stop=(k == KB - 1))
+                    finish(acc, LATE, b, first, width)
                     first += width

import concourse.mybir as mybir

F32, BF16, U16 = mybir.dt.float32, mybir.dt.bfloat16, mybir.dt.uint16
ADD = mybir.AluOpType.add
COPY = mybir.ActivationFunctionType.Copy
IDENTITY = mybir.ActivationFunctionType.Identity

P = 128
C = 512
M = 1536
S = 2048
GRID = 32
N = GRID * GRID
BANK = 512
BANKS = 8
SHORT = 128
HALF = BANK // 2
KB = C // P
JB = N // BANK

EARLY, LATE = 0, 1
GROUPS = 2
ROWS = M // GROUPS
BLOCKS = ROWS // P
LENT = 2
assert (KB - 2) * LENT == BLOCKS * JB - BANKS

FLOPS = 2 * C * M * N


def tile_autoregressivemodel_kernel(tc, table, row_embed, col_embed, wqkv, bqkv, offs, out):
    nc = tc.nc
    with (
        tc.tile_pool(name="held", bufs=1) as held,
        tc.tile_pool(name="staging", bufs=GROUPS * BLOCKS * JB + 2) as staging,
        tc.psum_pool(name="psum", bufs=BANKS) as psum,
    ):
        codes = held.tile([P, KB, GRID], F32, name="codes")
        nc.scalar.dma_start(codes[:, 0 : KB // 2, :], row_embed.rearrange("(k p) g -> p k g", p=P))
        nc.scalar.dma_start(codes[:, KB // 2 : KB, :], col_embed.rearrange("(k p) g -> p k g", p=P))

        offsets = held.tile([P, N // 16], U16, name="offsets")
        nc.sync.dma_start(offsets[:], offs)
        tables = [held.tile([P, S], F32, name=f"table{k}") for k in range(KB)]
        weights = [[held.tile([P, ROWS], BF16, name=f"weights{g}_{k}") for k in range(KB)] for g in range(GROUPS)]
        for k in range(KB):
            nc.sync.dma_start(tables[k][:], table[k * P : (k + 1) * P, :])
            nc.sync.dma_start(weights[EARLY][k][:], wqkv[k * P : (k + 1) * P, 0:ROWS])
        bias = held.tile([P, GROUPS, BLOCKS], F32, name="bias")
        nc.sync.dma_start(bias[:], bqkv.rearrange("(g p b) o -> p g (b o)", g=GROUPS, b=BLOCKS))
        for k in range(KB):
            nc.sync.dma_start(weights[LATE][k][:], wqkv[k * P : (k + 1) * P, ROWS:M])

        def stationary(g, b, k):
            return weights[g][k][:].rearrange("c (p b) -> c b p", b=BLOCKS)[:, b, :]

        out_of = out[C : C + M, :].rearrange("(g p b) n -> g b p n", g=GROUPS, b=BLOCKS)

        positions = []
        for k in range(KB):
            pos = held.tile([P, N], F32, name=f"pos{k}")
            pos_grid = pos[:].rearrange("p (r c) -> p r c", c=GRID)
            if k < KB // 2:
                nc.scalar.activation(pos_grid, codes[:, k, :].unsqueeze(2).to_broadcast([P, GRID, GRID]), COPY)
            else:
                nc.gpsimd.tensor_copy(pos_grid, codes[:, k, :].unsqueeze(1).to_broadcast([P, GRID, GRID]))
            positions.append(pos)

        h = held.tile([P, KB, N], F32, name="h")
        h_bf16 = [held.tile([P, N], BF16, name=f"h_bf16_{k}") for k in range(KB)]

        def embed(k, first, width):
            tokens = slice(first, first + width)
            nc.vector.tensor_tensor(
                h[:, k, tokens],
                tables[k][:].indirect(offsets[:, first // 16 : (first + width) // 16]),
                positions[k][:, tokens],
                ADD,
            )
            nc.scalar.activation(h_bf16[k][:, tokens], h[:, k, tokens], COPY)

        def project(acc, g, b, k, first, width, start, stop):
            nc.tensor.matmul(
                acc,
                stationary(g, b, k),
                h_bf16[k][:, first : first + width],
                start=start,
                stop=stop,
            )

        def finish(acc, g, b, first, width):
            qkv = staging.tile([P, width], F32, name="qkv")
            bias_b = bias[:, g, b : b + 1]
            if (b + first // BANK) % 2 == 0:
                nc.scalar.activation(qkv[:], acc[:], IDENTITY, bias=bias_b)
            else:
                nc.vector.tensor_scalar_add(qkv[:], acc[:], bias_b)
            nc.sync.dma_start(out_of[g, b, :, first : first + width], qkv[:])

        early = [(j, b) for j in range(JB) for b in range(BLOCKS)]
        sums = {}
        for j, b in early[:BANKS]:
            sums[j, b] = psum.tile([P, BANK], F32, name="acc")
        waiting = early[BANKS:]
        parked = []
        for k in range(KB):
            last = k == KB - 1
            leaving = [] if k == 0 or last else early[(k - 1) * LENT : k * LENT]
            first = 0
            while first < N:
                width = max(first, SHORT) if k == 0 else HALF if k == 1 else BANK
                embed(k, first, width)
                j, column = divmod(first, BANK)
                for b in range(BLOCKS):
                    if (j, b) in sums:
                        closes = (last or (j, b) in leaving) and column + width == BANK
                        project(
                            sums[j, b][:, column : column + width], EARLY, b, k, first, width,
                            start=(k == 0 and column == 0), stop=closes,
                        )
                first += width
            nc.sync.dma_start(out[k * P : (k + 1) * P, :], h[:, k, :])
            for j, b in leaving:
                part = held.tile([P, BANK], F32, name=f"part{j}_{b}")
                nc.scalar.activation(part[:], sums.pop((j, b))[:], COPY)
                parked.append((part, j, b, k + 1))
                j_next, b_next = waiting.pop(0)
                acc = psum.tile([P, BANK], F32, name="acc")
                for i in range(k + 1):
                    project(acc[:], EARLY, b_next, i, j_next * BANK, BANK, start=(i == 0), stop=False)
                sums[j_next, b_next] = acc

        for j, b in sums:
            finish(sums[j, b], EARLY, b, j * BANK, BANK)
        for part, j, b, first_missing in parked:
            acc = psum.tile([P, BANK], F32, name="acc")
            for k in range(first_missing, KB):
                project(acc[:], EARLY, b, k, j * BANK, BANK, start=(k == first_missing), stop=(k == KB - 1))
            qkv = staging.tile([P, BANK], F32, name="qkv")
            nc.vector.scalar_tensor_tensor(qkv[:], acc[:], bias[:, EARLY, b : b + 1], part[:], ADD, ADD)
            nc.sync.dma_start(out_of[EARLY, b, :, j * BANK : (j + 1) * BANK], qkv[:])

        for b in range(BLOCKS):
            for j in range(JB):
                final = (b, j) == (BLOCKS - 1, JB - 1)
                first, end = j * BANK, (j + 1) * BANK
                while first < end:
                    width = max((end - first) // 2, SHORT) if final else BANK
                    acc = psum.tile([P, width], F32, name="acc")
                    for k in range(KB):
                        project(acc[:], LATE, b, k, first, width, start=(k == 0), stop=(k == KB - 1))
                    finish(acc, LATE, b, first, width)
                    first += width
